import numpy as np
import ml_dtypes


def mxq(x, axis, fmt="e4m3"):
    dtype, down = {"e4m3": (ml_dtypes.float8_e4m3fn, 7), "e5m2": (ml_dtypes.float8_e5m2, 14)}[fmt]
    v = np.moveaxis(np.asarray(x, np.float32).astype(ml_dtypes.bfloat16).astype(np.float64), axis, -1)
    blocks = v.reshape(v.shape[:-1] + (-1, 32))
    amax = np.abs(blocks).max(-1, keepdims=True)
    byte = np.maximum(np.where(amax > 0, np.frexp(amax)[1] - 1 + 127, 0) - down, 1)
    scale = np.exp2(byte - 127.0)
    codes = (blocks / scale).astype(np.float32).astype(dtype).astype(np.float64)
    return np.moveaxis((codes * scale).reshape(v.shape), -1, axis)


WIDE = False


def mx_kscale(k):
    if not WIDE:
        return np.ones(k)
    levels = np.array([10, -10, 5, -5, 0])
    if k % 512:
        return np.exp2(np.random.permutation(np.resize(levels, k // 32))).repeat(32)
    a = np.empty((k // 512, 16))
    for p in range(k // 512):
        a[p, :8] = np.random.permutation(np.resize(levels, 8))
        for g in range(8):
            far = levels[np.abs(levels - a[p, g]) >= 10]
            a[p, g + 8] = far[np.random.randint(len(far))]
    return np.exp2(a.ravel()).repeat(32)


BF16 = ml_dtypes.bfloat16


def bf(x):
    return np.asarray(x, np.float32).astype(BF16)


def f64(x):
    return np.asarray(x).astype(np.float64)


B, S, D, N, A, F = 64, 64, 512, 128, 128, 512
LN_EPS = 1e-5


def setup_inputs():
    t = mx_kscale(F)
    return {
        "actions": bf(np.random.standard_normal((B, N, A))),
        "W_ae": bf(np.random.standard_normal((F, A)) / np.sqrt(A)),
        "b_ae": bf(np.random.standard_normal(F) * 0.4),
        "ln_g": bf((1.0 + 0.1 * np.random.standard_normal(F)) * t),
        "ln_b": bf(0.2 * np.random.standard_normal(F) * t),
        "Wv": bf(np.random.standard_normal((F, F)) / np.sqrt(F) / t[None, :]),
    }


def reference(actions, W_ae, b_ae, ln_g, ln_b, Wv):
    a = f64(actions) @ f64(W_ae).T + f64(b_ae)
    mu = a.mean(-1, keepdims=True)
    var = ((a - mu) ** 2).mean(-1, keepdims=True)
    a_n = (a - mu) / np.sqrt(var + LN_EPS) * f64(ln_g) + f64(ln_b)
    a_n = a_n
    return mxq(a_n, 2, "e4m3") @ mxq(f64(Wv), 1, "e4m3").T

@@ -1,0 +1,292 @@
+from contextlib import ExitStack
+
+import concourse.mybir as mybir
+from concourse.masks import make_identity
+
+BF16 = mybir.dt.bfloat16
+F32 = mybir.dt.float32
+U32 = mybir.dt.uint32
+U8 = mybir.dt.uint8
+FP8X4 = mybir.dt.float8_e4m3fn_x4
+ACT = mybir.ActivationFunctionType
+ALU = mybir.AluOpType
+
+P = 128
+PACK = 4
+TOKENS = 64 * 128
+A = 128
+F = 512
+O = 512
+TILES = TOKENS // P
+GROUP = 4
+GROUPS = TILES // GROUP
+GROUP_TOKENS = GROUP * P
+LOAD_CHUNKS = 4
+RUN = 4
+LN_EPS = 1e-5
+
+SQUARE_LAG = 2
+DEVIATION_LAG = SQUARE_LAG + GROUP - 1
+NORMALISE_LAG = 6
+FLIP_LAG = 10
+PACK_LAG = NORMALISE_LAG + 3 * GROUP
+PROJECT_LAG = PACK_LAG + 2
+STEPS = TILES + PROJECT_LAG
+SCALAR_BANKS = (1, 2)
+PREPARE_STEP = 4
+
+FLOPS = 2 * TOKENS * A * F + 2 * TOKENS * F * O
+
+
+def block(i):
+    return slice(i * P, (i + 1) * P)
+
+
+def tile_due(step, lag):
+    k = step - lag
+    return divmod(k, GROUP) if 0 <= k < TILES else None
+
+
+def group_due(step, lag):
+    due = tile_due(step, lag)
+    return due[0] if due is not None and due[1] == 0 else None
+
+
+def tile_actionbindingattention_pa_kernel(tc, actions, W_ae, b_ae, ln_g, ln_b, Wv, out):
+    nc = tc.nc
+    x_dram = actions.flatten_outer_dims().rearrange("(p n) a -> p n a", n=TILES)
+    out_dram = out.flatten_outer_dims().rearrange("(p n) o -> p n o", n=TILES)
+
+    with ExitStack() as ctx:
+        keep = ctx.enter_context(tc.tile_pool(name="keep", bufs=1))
+        work = ctx.enter_context(tc.tile_pool(name="work", bufs=3))
+        small = ctx.enter_context(tc.tile_pool(name="small", bufs=4))
+        results = ctx.enter_context(tc.tile_pool(name="results", bufs=8))
+        ps_bf = ctx.enter_context(tc.psum_pool(name="ps_bf", bufs=2))
+        ps_a = ctx.enter_context(tc.psum_pool(name="ps_a", bufs=2))
+        ps_z = ctx.enter_context(tc.psum_pool(name="ps_z", bufs=2))
+        ps_o = ctx.enter_context(tc.psum_pool(name="ps_o", bufs=2))
+        ctx.enter_context(tc.manual_schedule())
+
+        w_ae_sb = keep.tile([P, PACK, A], BF16)
+        nc.sync.dma_start(out=w_ae_sb[:], in_=W_ae.rearrange("(p j) a -> p j a", j=PACK))
+        bias_row = keep.tile([P, F], BF16)
+        nc.vector.memset(bias_row[:], 0.0)
+        nc.sync.dma_start(out=bias_row[0:1, :], in_=b_ae.rearrange("(o f) -> o f", o=1))
+        x_all = keep.tile([P, TILES, A], BF16)
+        chunk = TILES // LOAD_CHUNKS
+        nc.sync.dma_start(out=x_all[:, 0:chunk, :], in_=x_dram[:, 0:chunk, :])
+        gain_bf = keep.tile([P, PACK], BF16)
+        nc.sync.dma_start(out=gain_bf[:], in_=ln_g.rearrange("(p j) -> p j", j=PACK))
+        shift_bf = keep.tile([P, PACK], BF16)
+        nc.sync.dma_start(out=shift_bf[:], in_=ln_b.rearrange("(p j) -> p j", j=PACK))
+        wv_sb = keep.tile([P, O // P, F], BF16)
+        nc.sync.dma_start(out=wv_sb[:], in_=Wv.rearrange("(b r) f -> r b f", r=P))
+        for c in range(1, LOAD_CHUNKS):
+            rows = slice(c * chunk, (c + 1) * chunk)
+            nc.sync.dma_start(out=x_all[:, rows, :], in_=x_dram[:, rows, :])
+
+        ident_bf = keep.tile([P, P], BF16)
+        make_identity(nc, ident_bf[:])
+        ident_f32 = keep.tile([P, P], F32)
+        make_identity(nc, ident_f32[:])
+        ones_bf = keep.tile([P, P], BF16)
+        nc.vector.memset(ones_bf[:], 1.0)
+        eps = keep.tile([P, 1], F32)
+        nc.vector.memset(eps[:], LN_EPS)
+        table_warmer = keep.tile([P, 1], F32)
+        nc.scalar.activation(out=table_warmer[:], in_=eps[:], func=ACT.Sqrt)
+
+        w_aeT_ps = ps_bf.tile([P, F], BF16, tag="bf")
+        for j in range(PACK):
+            nc.tensor.transpose(out=w_aeT_ps[:, block(j)], in_=w_ae_sb[:, j, :], identity=ident_bf[:])
+        w_aeT = keep.tile([P, F], BF16)
+        nc.vector.tensor_copy(out=w_aeT[:], in_=w_aeT_ps[:])
+
+        bias_ps = ps_a.tile([P, F], F32, tag="a_ps")
+        nc.tensor.matmul(out=bias_ps[:], lhsT=ones_bf[:], rhs=bias_row[:], start=True, stop=True)
+        bias_bc = keep.tile([P, F], F32)
+        nc.vector.tensor_copy(
+            out=bias_bc[:].rearrange("r (j p) -> r j p", j=PACK), in_=bias_ps[:].rearrange("r (p j) -> r j p", j=PACK)
+        )
+
+        gain = keep.tile([P, PACK], F32)
+        shift = keep.tile([P, PACK], F32)
+        wv_grouped = keep.tile([P, O, PACK], BF16, align_bytes=64)
+        wv_codes = keep.tile([P, O], U32, align_bytes=64)
+        wv_scales = keep.tile([P, O], U8, align_bytes=64)
+
+        def widen_gain_shift():
+            nc.vector.tensor_copy(out=gain[:], in_=gain_bf[:])
+            nc.vector.tensor_copy(out=shift[:], in_=shift_bf[:])
+
+        def transpose_wv(b):
+            wvT_ps = ps_bf.tile([P, PACK, P], BF16, tag="bf")
+            planes = wv_sb[:, b, :].rearrange("r (p j) -> r j p", j=PACK)
+            for j in range(PACK):
+                nc.tensor.transpose(out=wvT_ps[:, j, :], in_=planes[:, j, :], identity=ident_bf[:])
+            nc.vector.tensor_copy(out=wv_grouped[:, block(b), :], in_=wvT_ps[:].rearrange("p j o -> p o j"))
+
+        def quantise_wv():
+            nc.vector.quantize_mx(
+                out=wv_codes[:].bitcast(FP8X4),
+                scales=wv_scales[:],
+                in_=wv_grouped[:].rearrange("p o j -> p (o j)"),
+            )
+
+        xT, a_sb, a_sum, dev_sq_sum, std, z_sb = {}, {}, {}, {}, {}, {}
+        a_n_planes, a_n_grouped, a_n_codes, a_n_scales = {}, {}, {}, {}
+
+        def transpose_actions(g):
+            xT_ps = ps_bf.tile([P, GROUP_TOKENS], BF16, tag="bf")
+            for n in range(GROUP):
+                nc.tensor.transpose(out=xT_ps[:, block(n)], in_=x_all[:, g * GROUP + n, :], identity=ident_bf[:])
+            xT_sb = work.tile([P, GROUP_TOKENS], BF16)
+            nc.scalar.copy(out=xT_sb[:], in_=xT_ps[:])
+            xT[g] = xT_sb
+
+        def encode(g, n):
+            if n == 0:
+                a_tile = work.tile([P, GROUP, F], F32)
+                a_sb[g] = a_tile
+                sum_tile = small.tile([P, GROUP], F32)
+                a_sum[g] = sum_tile
+            a_ps = ps_a.tile([P, F], F32)
+            nc.tensor.matmul(out=a_ps[:], lhsT=xT[g][:, block(n)], rhs=w_aeT[:], start=True, stop=True)
+            nc.vector.scalar_tensor_tensor(
+                out=a_sb[g][:, n, :],
+                in0=a_ps[:],
+                scalar=1.0,
+                in1=bias_bc[:],
+                op0=ALU.mult,
+                op1=ALU.add,
+                accum_out=a_sum[g][:, n : n + 1],
+            )
+
+        def square(g, n):
+            if n == 0:
+                sq_tile = small.tile([P, GROUP], F32)
+                dev_sq_sum[g] = sq_tile
+            dev_sq = work.tile([P, F], BF16)
+            nc.scalar.activation(
+                out=dev_sq[:],
+                in_=a_sb[g][:, n, :],
+                func=ACT.Square,
+                bias=a_sum[g][:, n : n + 1],
+                scale=-1.0 * F,
+                accum_out=dev_sq_sum[g][:, n : n + 1],
+            )
+
+        def deviation(g):
+            std_tile = small.tile([P, GROUP], F32)
+            nc.scalar.activation(
+                out=std_tile[:], in_=dev_sq_sum[g][:], func=ACT.Sqrt, bias=eps[:], scale=1.0 / (F * F * F)
+            )
+            std[g] = std_tile
+
+        def normalise(g):
+            rstd = small.tile([P, GROUP], F32)
+            nc.vector.reciprocal(out=rstd[:], in_=std[g][:])
+            neg_mean_rstd = small.tile([P, GROUP], F32)
+            nc.vector.scalar_tensor_tensor(
+                out=neg_mean_rstd[:], in0=a_sum[g][:], scalar=-1.0 / F, in1=rstd[:], op0=ALU.mult, op1=ALU.mult
+            )
+            z_tile = work.tile([P, GROUP, F], F32)
+            for n in range(GROUP):
+                nc.gpsimd.tensor_scalar(
+                    out=z_tile[:, n, :],
+                    in0=a_sb[g][:, n, :],
+                    scalar1=rstd[:, n : n + 1],
+                    scalar2=neg_mean_rstd[:, n : n + 1],
+                    op0=ALU.mult,
+                    op1=ALU.add,
+                )
+            z_sb[g] = z_tile
+
+        def flip(g, j):
+            if j == 0:
+                planes_tile = work.tile([P, PACK, GROUP_TOKENS], BF16)
+                a_n_planes[g] = planes_tile
+            zT_ps = ps_z.tile([P, GROUP_TOKENS], F32)
+            for n in range(GROUP):
+                nc.tensor.transpose(out=zT_ps[:, block(n)], in_=z_sb[g][:, n, block(j)], identity=ident_f32[:])
+            nc.scalar.activation(
+                out=a_n_planes[g][:, j, :],
+                in_=zT_ps[:],
+                func=ACT.Identity,
+                scale=gain[:, j : j + 1],
+                bias=shift[:, j : j + 1],
+            )
+
+        def regroup(g):
+            grouped_tile = work.tile([P, GROUP_TOKENS, PACK], BF16, align_bytes=64)
+            nc.vector.tensor_copy(
+                out=grouped_tile[:].rearrange("p (c i) j -> p c j i", i=RUN),
+                in_=a_n_planes[g][:].rearrange("p j (c i) -> p c j i", i=RUN),
+            )
+            a_n_grouped[g] = grouped_tile
+
+        def quantise(g):
+            codes_tile = work.tile([P, GROUP_TOKENS], U32, align_bytes=64)
+            scales_tile = work.tile([P, GROUP_TOKENS], U8, align_bytes=64)
+            nc.vector.quantize_mx(
+                out=codes_tile[:].bitcast(FP8X4),
+                scales=scales_tile[:],
+                in_=a_n_grouped[g][:].rearrange("p c j -> p (c j)"),
+            )
+            a_n_codes[g] = codes_tile
+            a_n_scales[g] = scales_tile
+
+        def project(g, n):
+            out_ps = ps_o.tile([P, O], F32)
+            nc.tensor.matmul_mx(
+                out=out_ps[:],
+                lhsT=a_n_codes[g][:, block(n)].bitcast(FP8X4),
+                lhsT_scale=a_n_scales[g][:, block(n)],
+                rhs=wv_codes[:].bitcast(FP8X4),
+                rhs_scale=wv_scales[:],
+                start=True,
+                stop=True,
+            )
+            out_sb = results.tile([P, O], F32)
+            if n in SCALAR_BANKS:
+                nc.scalar.copy(out=out_sb[:], in_=out_ps[:])
+            else:
+                nc.vector.tensor_copy(out=out_sb[:], in_=out_ps[:])
+            nc.sync.dma_start(out=out_dram[:, g * GROUP + n, :], in_=out_sb[:])
+
+        transpose_actions(0)
+        for step in range(STEPS):
+            packed = group_due(step, PACK_LAG)
+            if packed is not None:
+                regroup(packed)
+            due = tile_due(step, 0)
+            if due is not None:
+                encode(due[0], due[1])
+            if packed is not None:
+                quantise(packed)
+            g = group_due(step, 1 - GROUP)
+            if g is not None:
+                transpose_actions(g)
+            due = tile_due(step, SQUARE_LAG)
+            if due is not None:
+                square(due[0], due[1])
+            g = group_due(step, DEVIATION_LAG)
+            if g is not None:
+                deviation(g)
+            due = tile_due(step, FLIP_LAG)
+            if due is not None:
+                flip(due[0], due[1])
+            due = tile_due(step, PROJECT_LAG)
+            if due is not None:
+                project(due[0], due[1])
+            g = group_due(step, NORMALISE_LAG)
+            if g is not None:
+                normalise(g)
+            b = step - PREPARE_STEP
+            if b == 0:
+                widen_gain_shift()
+            if 0 <= b < O // P:
+                transpose_wv(b)
+            if b == O // P:
+                quantise_wv()

@@ -18,21 +18,27 @@ A = 128
 F = 512
 O = 512
 TILES = TOKENS // P
-GROUP = 4
+GROUP = 2
 GROUPS = TILES // GROUP
 GROUP_TOKENS = GROUP * P
-LOAD_CHUNKS = 4
+BANK = 512
+BANK_PLANES = BANK // GROUP_TOKENS
+LOAD_TILES = (4, 12, 16, 16, 16)
 RUN = 4
 LN_EPS = 1e-5
 
-SQUARE_LAG = 2
+TURN_LAG = -4
+ENCODE_LAG = -1
+SQUARE_LAG = 1
 DEVIATION_LAG = SQUARE_LAG + GROUP - 1
-NORMALISE_LAG = 6
-FLIP_LAG = 10
-PACK_LAG = NORMALISE_LAG + 3 * GROUP
-PROJECT_LAG = PACK_LAG + 2
+NORMALISE_LAG = 5
+FLIP_LAG = 7
+REGROUP_LAG = 11
+QUANTISE_LAG = NORMALISE_LAG + 4 * GROUP
+PROJECT_LAG = QUANTISE_LAG + GROUP
 STEPS = TILES + PROJECT_LAG
-SCALAR_BANKS = (1, 2)
+VECTOR_BANKS = (0,)
+VECTOR_OUTPUTS = 8
 PREPARE_STEP = 4
 
 FLOPS = 2 * TOKENS * A * F + 2 * TOKENS * F * O
@@ -43,13 +49,13 @@ def block(i):
 
 
 def tile_due(step, lag):
-    k = step - lag
-    return divmod(k, GROUP) if 0 <= k < TILES else None
+    i = step - lag
+    return i if 0 <= i < TILES else None
 
 
 def group_due(step, lag):
-    due = tile_due(step, lag)
-    return due[0] if due is not None and due[1] == 0 else None
+    i = tile_due(step, lag)
+    return i // GROUP if i is not None and i % GROUP == 0 else None
 
 
 def tile_actionbindingattention_pa_kernel(tc, actions, W_ae, b_ae, ln_g, ln_b, Wv, out):
@@ -59,56 +65,58 @@ def tile_actionbindingattention_pa_kernel(tc, actions, W_ae, b_ae, ln_g, ln_b, W
 
     with ExitStack() as ctx:
         keep = ctx.enter_context(tc.tile_pool(name="keep", bufs=1))
-        work = ctx.enter_context(tc.tile_pool(name="work", bufs=3))
-        small = ctx.enter_context(tc.tile_pool(name="small", bufs=4))
+        work = ctx.enter_context(tc.tile_pool(name="work", bufs=4))
+        small = ctx.enter_context(tc.tile_pool(name="small", bufs=6))
         results = ctx.enter_context(tc.tile_pool(name="results", bufs=8))
-        ps_bf = ctx.enter_context(tc.psum_pool(name="ps_bf", bufs=2))
-        ps_a = ctx.enter_context(tc.psum_pool(name="ps_a", bufs=2))
-        ps_z = ctx.enter_context(tc.psum_pool(name="ps_z", bufs=2))
-        ps_o = ctx.enter_context(tc.psum_pool(name="ps_o", bufs=2))
+        ps_a = ctx.enter_context(tc.psum_pool(name="ps_a", bufs=3))
+        ps_t = ctx.enter_context(tc.psum_pool(name="ps_t", bufs=2))
+        ps_o = ctx.enter_context(tc.psum_pool(name="ps_o", bufs=3))
         ctx.enter_context(tc.manual_schedule())
 
         w_ae_sb = keep.tile([P, PACK, A], BF16)
         nc.sync.dma_start(out=w_ae_sb[:], in_=W_ae.rearrange("(p j) a -> p j a", j=PACK))
-        bias_row = keep.tile([P, F], BF16)
-        nc.vector.memset(bias_row[:], 0.0)
-        nc.sync.dma_start(out=bias_row[0:1, :], in_=b_ae.rearrange("(o f) -> o f", o=1))
+        bias_bf = keep.tile([P, PACK], BF16)
+        nc.sync.dma_start(out=bias_bf[:], in_=b_ae.rearrange("(p j) -> p j", j=PACK))
         x_all = keep.tile([P, TILES, A], BF16)
-        chunk = TILES // LOAD_CHUNKS
-        nc.sync.dma_start(out=x_all[:, 0:chunk, :], in_=x_dram[:, 0:chunk, :])
+
+        def load_actions(c):
+            first = sum(LOAD_TILES[:c])
+            rows = slice(first, first + LOAD_TILES[c])
+            nc.sync.dma_start(out=x_all[:, rows, :], in_=x_dram[:, rows, :])
+
+        load_actions(0)
+        load_actions(1)
         gain_bf = keep.tile([P, PACK], BF16)
         nc.sync.dma_start(out=gain_bf[:], in_=ln_g.rearrange("(p j) -> p j", j=PACK))
         shift_bf = keep.tile([P, PACK], BF16)
         nc.sync.dma_start(out=shift_bf[:], in_=ln_b.rearrange("(p j) -> p j", j=PACK))
         wv_sb = keep.tile([P, O // P, F], BF16)
         nc.sync.dma_start(out=wv_sb[:], in_=Wv.rearrange("(b r) f -> r b f", r=P))
-        for c in range(1, LOAD_CHUNKS):
-            rows = slice(c * chunk, (c + 1) * chunk)
-            nc.sync.dma_start(out=x_all[:, rows, :], in_=x_dram[:, rows, :])
+        for c in range(2, len(LOAD_TILES)):
+            load_actions(c)
 
         ident_bf = keep.tile([P, P], BF16)
         make_identity(nc, ident_bf[:])
         ident_f32 = keep.tile([P, P], F32)
         make_identity(nc, ident_f32[:])
-        ones_bf = keep.tile([P, P], BF16)
-        nc.vector.memset(ones_bf[:], 1.0)
         eps = keep.tile([P, 1], F32)
         nc.vector.memset(eps[:], LN_EPS)
         table_warmer = keep.tile([P, 1], F32)
-        nc.scalar.activation(out=table_warmer[:], in_=eps[:], func=ACT.Sqrt)
+        nc.scalar.activation(out=table_warmer[:], in_=eps[:], func=ACT.Abs_reciprocal_sqrt)
 
-        w_aeT_ps = ps_bf.tile([P, F], BF16, tag="bf")
+        w_aeT_ps = ps_t.tile([P, F], BF16, tag="turned")
         for j in range(PACK):
             nc.tensor.transpose(out=w_aeT_ps[:, block(j)], in_=w_ae_sb[:, j, :], identity=ident_bf[:])
         w_aeT = keep.tile([P, F], BF16)
         nc.vector.tensor_copy(out=w_aeT[:], in_=w_aeT_ps[:])
 
+        bias_cols = keep.tile([P, PACK, P], F32)
+        nc.vector.tensor_copy(out=bias_cols[:], in_=bias_bf[:].unsqueeze(2).to_broadcast([P, PACK, P]))
         bias_ps = ps_a.tile([P, F], F32, tag="a_ps")
-        nc.tensor.matmul(out=bias_ps[:], lhsT=ones_bf[:], rhs=bias_row[:], start=True, stop=True)
+        for j in range(PACK):
+            nc.tensor.transpose(out=bias_ps[:, block(j)], in_=bias_cols[:, j, :], identity=ident_f32[:])
         bias_bc = keep.tile([P, F], F32)
-        nc.vector.tensor_copy(
-            out=bias_bc[:].rearrange("r (j p) -> r j p", j=PACK), in_=bias_ps[:].rearrange("r (p j) -> r j p", j=PACK)
-        )
+        nc.vector.tensor_copy(out=bias_bc[:], in_=bias_ps[:])
 
         gain = keep.tile([P, PACK], F32)
         shift = keep.tile([P, PACK], F32)
@@ -121,7 +129,7 @@ def tile_actionbindingattention_pa_kernel(tc, actions, W_ae, b_ae, ln_g, ln_b, W
             nc.vector.tensor_copy(out=shift[:], in_=shift_bf[:])
 
         def transpose_wv(b):
-            wvT_ps = ps_bf.tile([P, PACK, P], BF16, tag="bf")
+            wvT_ps = ps_t.tile([P, PACK, P], BF16, tag="turned")
             planes = wv_sb[:, b, :].rearrange("r (p j) -> r j p", j=PACK)
             for j in range(PACK):
                 nc.tensor.transpose(out=wvT_ps[:, j, :], in_=planes[:, j, :], identity=ident_bf[:])
@@ -134,28 +142,33 @@ def tile_actionbindingattention_pa_kernel(tc, actions, W_ae, b_ae, ln_g, ln_b, W
                 in_=wv_grouped[:].rearrange("p o j -> p (o j)"),
             )
 
-        xT, a_sb, a_sum, dev_sq_sum, std, z_sb = {}, {}, {}, {}, {}, {}
-        a_n_planes, a_n_grouped, a_n_codes, a_n_scales = {}, {}, {}, {}
+        xT, a_psum, a_sb, a_sum, dev_sq_sum, rstd, mean, z_sb = {}, {}, {}, {}, {}, {}, {}, {}
+        a_n_planes, a_n_grouped, a_n_codes, a_n_scales, out_psum = {}, {}, {}, {}, {}
 
         def transpose_actions(g):
-            xT_ps = ps_bf.tile([P, GROUP_TOKENS], BF16, tag="bf")
+            xT_ps = ps_t.tile([P, GROUP_TOKENS], BF16, tag="turned")
             for n in range(GROUP):
                 nc.tensor.transpose(out=xT_ps[:, block(n)], in_=x_all[:, g * GROUP + n, :], identity=ident_bf[:])
             xT_sb = work.tile([P, GROUP_TOKENS], BF16)
             nc.scalar.copy(out=xT_sb[:], in_=xT_ps[:])
             xT[g] = xT_sb
 
-        def encode(g, n):
+        def encode(i):
+            g, n = divmod(i, GROUP)
+            a_ps = ps_a.tile([P, F], F32)
+            nc.tensor.matmul(out=a_ps[:], lhsT=xT[g][:, block(n)], rhs=w_aeT[:], start=True, stop=True)
+            a_psum[i] = a_ps
+
+        def add_bias(i):
+            g, n = divmod(i, GROUP)
             if n == 0:
                 a_tile = work.tile([P, GROUP, F], F32)
                 a_sb[g] = a_tile
                 sum_tile = small.tile([P, GROUP], F32)
                 a_sum[g] = sum_tile
-            a_ps = ps_a.tile([P, F], F32)
-            nc.tensor.matmul(out=a_ps[:], lhsT=xT[g][:, block(n)], rhs=w_aeT[:], start=True, stop=True)
             nc.vector.scalar_tensor_tensor(
                 out=a_sb[g][:, n, :],
-                in0=a_ps[:],
+                in0=a_psum[i][:],
                 scalar=1.0,
                 in1=bias_bc[:],
                 op0=ALU.mult,
@@ -163,7 +176,8 @@ def tile_actionbindingattention_pa_kernel(tc, actions, W_ae, b_ae, ln_g, ln_b, W
                 accum_out=a_sum[g][:, n : n + 1],
             )
 
-        def square(g, n):
+        def square(i):
+            g, n = divmod(i, GROUP)
             if n == 0:
                 sq_tile = small.tile([P, GROUP], F32)
                 dev_sq_sum[g] = sq_tile
@@ -178,45 +192,65 @@ def tile_actionbindingattention_pa_kernel(tc, actions, W_ae, b_ae, ln_g, ln_b, W
             )
 
         def deviation(g):
-            std_tile = small.tile([P, GROUP], F32)
+            rstd_tile = small.tile([P, GROUP], F32)
             nc.scalar.activation(
-                out=std_tile[:], in_=dev_sq_sum[g][:], func=ACT.Sqrt, bias=eps[:], scale=1.0 / (F * F * F)
+                out=rstd_tile[:],
+                in_=dev_sq_sum[g][:],
+                func=ACT.Abs_reciprocal_sqrt,
+                bias=eps[:],
+                scale=1.0 / (F * F * F),
             )
-            std[g] = std_tile
+            rstd[g] = rstd_tile
+
+        def average(g):
+            mean_tile = small.tile([P, GROUP], F32)
+            nc.vector.tensor_scalar(out=mean_tile[:], in0=a_sum[g][:], scalar1=1.0 / F, scalar2=None, op0=ALU.mult)
+            mean[g] = mean_tile
 
         def normalise(g):
-            rstd = small.tile([P, GROUP], F32)
-            nc.vector.reciprocal(out=rstd[:], in_=std[g][:])
-            neg_mean_rstd = small.tile([P, GROUP], F32)
-            nc.vector.scalar_tensor_tensor(
-                out=neg_mean_rstd[:], in0=a_sum[g][:], scalar=-1.0 / F, in1=rstd[:], op0=ALU.mult, op1=ALU.mult
-            )
             z_tile = work.tile([P, GROUP, F], F32)
             for n in range(GROUP):
                 nc.gpsimd.tensor_scalar(
                     out=z_tile[:, n, :],
                     in0=a_sb[g][:, n, :],
-                    scalar1=rstd[:, n : n + 1],
-                    scalar2=neg_mean_rstd[:, n : n + 1],
-                    op0=ALU.mult,
-                    op1=ALU.add,
+                    scalar1=mean[g][:, n : n + 1],
+                    scalar2=rstd[g][:, n : n + 1],
+                    op0=ALU.subtract,
+                    op1=ALU.mult,
                 )
             z_sb[g] = z_tile
 
-        def flip(g, j):
-            if j == 0:
+        def flip(g, k):
+            if k == 0:
                 planes_tile = work.tile([P, PACK, GROUP_TOKENS], BF16)
                 a_n_planes[g] = planes_tile
-            zT_ps = ps_z.tile([P, GROUP_TOKENS], F32)
-            for n in range(GROUP):
-                nc.tensor.transpose(out=zT_ps[:, block(n)], in_=z_sb[g][:, n, block(j)], identity=ident_f32[:])
-            nc.scalar.activation(
-                out=a_n_planes[g][:, j, :],
-                in_=zT_ps[:],
-                func=ACT.Identity,
-                scale=gain[:, j : j + 1],
-                bias=shift[:, j : j + 1],
-            )
+            zT_ps = ps_t.tile([P, BANK_PLANES, GROUP_TOKENS], F32, tag="turned")
+            for b in range(BANK_PLANES):
+                for n in range(GROUP):
+                    nc.tensor.transpose(
+                        out=zT_ps[:, b, block(n)],
+                        in_=z_sb[g][:, n, block(k * BANK_PLANES + b)],
+                        identity=ident_f32[:],
+                    )
+            for b in range(BANK_PLANES):
+                j = k * BANK_PLANES + b
+                if k in VECTOR_BANKS:
+                    nc.vector.tensor_scalar(
+                        out=a_n_planes[g][:, j, :],
+                        in0=zT_ps[:, b, :],
+                        scalar1=gain[:, j : j + 1],
+                        scalar2=shift[:, j : j + 1],
+                        op0=ALU.mult,
+                        op1=ALU.add,
+                    )
+                else:
+                    nc.scalar.activation(
+                        out=a_n_planes[g][:, j, :],
+                        in_=zT_ps[:, b, :],
+                        func=ACT.Identity,
+                        scale=gain[:, j : j + 1],
+                        bias=shift[:, j : j + 1],
+                    )
 
         def regroup(g):
             grouped_tile = work.tile([P, GROUP_TOKENS, PACK], BF16, align_bytes=64)
@@ -237,7 +271,8 @@ def tile_actionbindingattention_pa_kernel(tc, actions, W_ae, b_ae, ln_g, ln_b, W
             a_n_codes[g] = codes_tile
             a_n_scales[g] = scales_tile
 
-        def project(g, n):
+        def project(i):
+            g, n = divmod(i, GROUP)
             out_ps = ps_o.tile([P, O], F32)
             nc.tensor.matmul_mx(
                 out=out_ps[:],
@@ -248,41 +283,54 @@ def tile_actionbindingattention_pa_kernel(tc, actions, W_ae, b_ae, ln_g, ln_b, W
                 start=True,
                 stop=True,
             )
-            out_sb = results.tile([P, O], F32)
-            if n in SCALAR_BANKS:
-                nc.scalar.copy(out=out_sb[:], in_=out_ps[:])
-            else:
-                nc.vector.tensor_copy(out=out_sb[:], in_=out_ps[:])
-            nc.sync.dma_start(out=out_dram[:, g * GROUP + n, :], in_=out_sb[:])
+            out_psum[i] = out_ps
 
-        transpose_actions(0)
-        for step in range(STEPS):
-            packed = group_due(step, PACK_LAG)
-            if packed is not None:
-                regroup(packed)
-            due = tile_due(step, 0)
-            if due is not None:
-                encode(due[0], due[1])
-            if packed is not None:
-                quantise(packed)
-            g = group_due(step, 1 - GROUP)
+        def store(i):
+            out_sb = results.tile([P, O], F32)
+            if i % VECTOR_OUTPUTS == 3:
+                nc.vector.tensor_copy(out=out_sb[:], in_=out_psum[i][:])
+            else:
+                nc.scalar.copy(out=out_sb[:], in_=out_psum[i][:])
+            nc.sync.dma_start(out=out_dram[:, i, :], in_=out_sb[:])
+
+        for step in range(TURN_LAG, STEPS):
+            g = group_due(step, REGROUP_LAG)
+            if g is not None:
+                regroup(g)
+            g = group_due(step, QUANTISE_LAG)
+            if g is not None:
+                quantise(g)
+            g = group_due(step, NORMALISE_LAG)
+            if g is not None:
+                average(g)
+            g = group_due(step, PROJECT_LAG)
+            if g is not None:
+                for n in range(GROUP):
+                    project(g * GROUP + n)
+            i = tile_due(step, 0)
+            if i is not None:
+                add_bias(i)
+            g = group_due(step, TURN_LAG)
             if g is not None:
                 transpose_actions(g)
-            due = tile_due(step, SQUARE_LAG)
-            if due is not None:
-                square(due[0], due[1])
+            i = tile_due(step, SQUARE_LAG)
+            if i is not None:
+                square(i)
+            i = tile_due(step, PROJECT_LAG)
+            if i is not None:
+                store(i)
+            i = tile_due(step, FLIP_LAG)
+            if i is not None:
+                flip(i // GROUP, i % GROUP)
             g = group_due(step, DEVIATION_LAG)
             if g is not None:
                 deviation(g)
-            due = tile_due(step, FLIP_LAG)
-            if due is not None:
-                flip(due[0], due[1])
-            due = tile_due(step, PROJECT_LAG)
-            if due is not None:
-                project(due[0], due[1])
             g = group_due(step, NORMALISE_LAG)
             if g is not None:
                 normalise(g)
+            i = tile_due(step, ENCODE_LAG)
+            if i is not None:
+                encode(i)
             b = step - PREPARE_STEP
             if b == 0:
                 widen_gain_shift()

@@ -142,7 +142,7 @@ def tile_actionbindingattention_pa_kernel(tc, actions, W_ae, b_ae, ln_g, ln_b, W
                 in_=wv_grouped[:].rearrange("p o j -> p (o j)"),
             )
 
-        xT, a_psum, a_sb, a_sum, dev_sq_sum, rstd, mean, z_sb = {}, {}, {}, {}, {}, {}, {}, {}
+        xT, a_psum, a_sb, a_sum, dev_sq_sum, rstd, neg_mean_rstd, z_sb = {}, {}, {}, {}, {}, {}, {}, {}
         a_n_planes, a_n_grouped, a_n_codes, a_n_scales, out_psum = {}, {}, {}, {}, {}
 
         def transpose_actions(g):
@@ -202,10 +202,12 @@ def tile_actionbindingattention_pa_kernel(tc, actions, W_ae, b_ae, ln_g, ln_b, W
             )
             rstd[g] = rstd_tile
 
-        def average(g):
-            mean_tile = small.tile([P, GROUP], F32)
-            nc.vector.tensor_scalar(out=mean_tile[:], in0=a_sum[g][:], scalar1=1.0 / F, scalar2=None, op0=ALU.mult)
-            mean[g] = mean_tile
+        def centre(g):
+            centre_tile = small.tile([P, GROUP], F32)
+            nc.vector.scalar_tensor_tensor(
+                out=centre_tile[:], in0=a_sum[g][:], scalar=-1.0 / F, in1=rstd[g][:], op0=ALU.mult, op1=ALU.mult
+            )
+            neg_mean_rstd[g] = centre_tile
 
         def normalise(g):
             z_tile = work.tile([P, GROUP, F], F32)
@@ -213,10 +215,10 @@ def tile_actionbindingattention_pa_kernel(tc, actions, W_ae, b_ae, ln_g, ln_b, W
                 nc.gpsimd.tensor_scalar(
                     out=z_tile[:, n, :],
                     in0=a_sb[g][:, n, :],
-                    scalar1=mean[g][:, n : n + 1],
-                    scalar2=rstd[g][:, n : n + 1],
-                    op0=ALU.subtract,
-                    op1=ALU.mult,
+                    scalar1=rstd[g][:, n : n + 1],
+                    scalar2=neg_mean_rstd[g][:, n : n + 1],
+                    op0=ALU.mult,
+                    op1=ALU.add,
                 )
             z_sb[g] = z_tile
 
@@ -302,7 +304,7 @@ def tile_actionbindingattention_pa_kernel(tc, actions, W_ae, b_ae, ln_g, ln_b, W
                 quantise(g)
             g = group_due(step, NORMALISE_LAG)
             if g is not None:
-                average(g)
+                centre(g)
             g = group_due(step, PROJECT_LAG)
             if g is not None:
                 for n in range(GROUP):

@@ -23,23 +23,25 @@ GROUPS = TILES // GROUP
 GROUP_TOKENS = GROUP * P
 BANK = 512
 BANK_PLANES = BANK // GROUP_TOKENS
-LOAD_TILES = (4, 12, 16, 16, 16)
+LOAD_TILES = (4, 4, 8, 16, 16, 16)
 RUN = 4
 LN_EPS = 1e-5
 
-TURN_LAG = -4
+TURN_LAG = -3
 ENCODE_LAG = -1
 SQUARE_LAG = 1
 DEVIATION_LAG = SQUARE_LAG + GROUP - 1
-NORMALISE_LAG = 5
-FLIP_LAG = 7
-REGROUP_LAG = 11
+NORMALISE_LAG = DEVIATION_LAG + 2
+FLIP_LAG = NORMALISE_LAG + 3
+REGROUP_LAG = FLIP_LAG + 3
 QUANTISE_LAG = NORMALISE_LAG + 4 * GROUP
-PROJECT_LAG = QUANTISE_LAG + GROUP
+PROJECT_LAG = QUANTISE_LAG + 2
 STEPS = TILES + PROJECT_LAG
-VECTOR_BANKS = (0,)
-VECTOR_OUTPUTS = 8
-PREPARE_STEP = 4
+VECTOR_BANKS = (1,)
+SCALAR_GROUPS = 2
+VECTOR_OUTPUTS = 16
+PREPARE_STEP = 3
+SCALAR_WV = (0, 2)
 
 FLOPS = 2 * TOKENS * A * F + 2 * TOKENS * F * O
 
@@ -68,15 +70,15 @@ def tile_actionbindingattention_pa_kernel(tc, actions, W_ae, b_ae, ln_g, ln_b, W
         work = ctx.enter_context(tc.tile_pool(name="work", bufs=4))
         small = ctx.enter_context(tc.tile_pool(name="small", bufs=6))
         results = ctx.enter_context(tc.tile_pool(name="results", bufs=8))
-        ps_a = ctx.enter_context(tc.psum_pool(name="ps_a", bufs=3))
-        ps_t = ctx.enter_context(tc.psum_pool(name="ps_t", bufs=2))
+        ps_a = ctx.enter_context(tc.psum_pool(name="ps_a", bufs=2))
+        ps_t = ctx.enter_context(tc.psum_pool(name="ps_t", bufs=3))
         ps_o = ctx.enter_context(tc.psum_pool(name="ps_o", bufs=3))
         ctx.enter_context(tc.manual_schedule())
 
-        w_ae_sb = keep.tile([P, PACK, A], BF16)
-        nc.sync.dma_start(out=w_ae_sb[:], in_=W_ae.rearrange("(p j) a -> p j a", j=PACK))
         bias_bf = keep.tile([P, PACK], BF16)
         nc.sync.dma_start(out=bias_bf[:], in_=b_ae.rearrange("(p j) -> p j", j=PACK))
+        w_ae_sb = keep.tile([P, PACK, A], BF16)
+        nc.sync.dma_start(out=w_ae_sb[:], in_=W_ae.rearrange("(p j) a -> p j a", j=PACK))
         x_all = keep.tile([P, TILES, A], BF16)
 
         def load_actions(c):
@@ -85,30 +87,24 @@ def tile_actionbindingattention_pa_kernel(tc, actions, W_ae, b_ae, ln_g, ln_b, W
             nc.sync.dma_start(out=x_all[:, rows, :], in_=x_dram[:, rows, :])
 
         load_actions(0)
-        load_actions(1)
         gain_bf = keep.tile([P, PACK], BF16)
         nc.sync.dma_start(out=gain_bf[:], in_=ln_g.rearrange("(p j) -> p j", j=PACK))
         shift_bf = keep.tile([P, PACK], BF16)
         nc.sync.dma_start(out=shift_bf[:], in_=ln_b.rearrange("(p j) -> p j", j=PACK))
+        load_actions(1)
         wv_sb = keep.tile([P, O // P, F], BF16)
         nc.sync.dma_start(out=wv_sb[:], in_=Wv.rearrange("(b r) f -> r b f", r=P))
         for c in range(2, len(LOAD_TILES)):
             load_actions(c)
 
-        ident_bf = keep.tile([P, P], BF16)
-        make_identity(nc, ident_bf[:])
         ident_f32 = keep.tile([P, P], F32)
         make_identity(nc, ident_f32[:])
+        ident_bf = keep.tile([P, P], BF16)
+        make_identity(nc, ident_bf[:])
         eps = keep.tile([P, 1], F32)
         nc.vector.memset(eps[:], LN_EPS)
         table_warmer = keep.tile([P, 1], F32)
         nc.scalar.activation(out=table_warmer[:], in_=eps[:], func=ACT.Abs_reciprocal_sqrt)
-
-        w_aeT_ps = ps_t.tile([P, F], BF16, tag="turned")
-        for j in range(PACK):
-            nc.tensor.transpose(out=w_aeT_ps[:, block(j)], in_=w_ae_sb[:, j, :], identity=ident_bf[:])
-        w_aeT = keep.tile([P, F], BF16)
-        nc.vector.tensor_copy(out=w_aeT[:], in_=w_aeT_ps[:])
 
         bias_cols = keep.tile([P, PACK, P], F32)
         nc.vector.tensor_copy(out=bias_cols[:], in_=bias_bf[:].unsqueeze(2).to_broadcast([P, PACK, P]))
@@ -116,7 +112,13 @@ def tile_actionbindingattention_pa_kernel(tc, actions, W_ae, b_ae, ln_g, ln_b, W
         for j in range(PACK):
             nc.tensor.transpose(out=bias_ps[:, block(j)], in_=bias_cols[:, j, :], identity=ident_f32[:])
         bias_bc = keep.tile([P, F], F32)
-        nc.vector.tensor_copy(out=bias_bc[:], in_=bias_ps[:])
+        nc.scalar.copy(out=bias_bc[:], in_=bias_ps[:])
+
+        w_aeT_ps = ps_t.tile([P, F], BF16, tag="turned")
+        for j in range(PACK):
+            nc.tensor.transpose(out=w_aeT_ps[:, block(j)], in_=w_ae_sb[:, j, :], identity=ident_bf[:])
+        w_aeT = keep.tile([P, F], BF16)
+        nc.vector.tensor_copy(out=w_aeT[:], in_=w_aeT_ps[:])
 
         gain = keep.tile([P, PACK], F32)
         shift = keep.tile([P, PACK], F32)
@@ -133,7 +135,11 @@ def tile_actionbindingattention_pa_kernel(tc, actions, W_ae, b_ae, ln_g, ln_b, W
             planes = wv_sb[:, b, :].rearrange("r (p j) -> r j p", j=PACK)
             for j in range(PACK):
                 nc.tensor.transpose(out=wvT_ps[:, j, :], in_=planes[:, j, :], identity=ident_bf[:])
-            nc.vector.tensor_copy(out=wv_grouped[:, block(b), :], in_=wvT_ps[:].rearrange("p j o -> p o j"))
+            by_word = wvT_ps[:].rearrange("p j o -> p o j")
+            if b in SCALAR_WV:
+                nc.scalar.copy(out=wv_grouped[:, block(b), :], in_=by_word)
+            else:
+                nc.vector.tensor_copy(out=wv_grouped[:, block(b), :], in_=by_word)
 
         def quantise_wv():
             nc.vector.quantize_mx(
@@ -236,7 +242,7 @@ def tile_actionbindingattention_pa_kernel(tc, actions, W_ae, b_ae, ln_g, ln_b, W
                     )
             for b in range(BANK_PLANES):
                 j = k * BANK_PLANES + b
-                if k in VECTOR_BANKS:
+                if k in VECTOR_BANKS and g >= SCALAR_GROUPS:
                     nc.vector.tensor_scalar(
                         out=a_n_planes[g][:, j, :],
                         in0=zT_ps[:, b, :],
@@ -289,7 +295,7 @@ def tile_actionbindingattention_pa_kernel(tc, actions, W_ae, b_ae, ln_g, ln_b, W
 
         def store(i):
             out_sb = results.tile([P, O], F32)
-            if i % VECTOR_OUTPUTS == 3:
+            if i % VECTOR_OUTPUTS == VECTOR_OUTPUTS - 1:
                 nc.vector.tensor_copy(out=out_sb[:], in_=out_psum[i][:])
             else:
                 nc.scalar.copy(out=out_sb[:], in_=out_psum[i][:])
@@ -305,10 +311,9 @@ def tile_actionbindingattention_pa_kernel(tc, actions, W_ae, b_ae, ln_g, ln_b, W
             g = group_due(step, NORMALISE_LAG)
             if g is not None:
                 centre(g)
-            g = group_due(step, PROJECT_LAG)
-            if g is not None:
-                for n in range(GROUP):
-                    project(g * GROUP + n)
+            i = tile_due(step, PROJECT_LAG)
+            if i is not None:
+                project(i)
             i = tile_due(step, 0)
             if i is not None:
                 add_bias(i)

@@ -75,10 +75,10 @@ def tile_actionbindingattention_pa_kernel(tc, actions, W_ae, b_ae, ln_g, ln_b, W
         ps_o = ctx.enter_context(tc.psum_pool(name="ps_o", bufs=3))
         ctx.enter_context(tc.manual_schedule())
 
-        bias_bf = keep.tile([P, PACK], BF16)
-        nc.sync.dma_start(out=bias_bf[:], in_=b_ae.rearrange("(p j) -> p j", j=PACK))
         w_ae_sb = keep.tile([P, PACK, A], BF16)
         nc.sync.dma_start(out=w_ae_sb[:], in_=W_ae.rearrange("(p j) a -> p j a", j=PACK))
+        bias_bf = keep.tile([P, PACK], BF16)
+        nc.sync.dma_start(out=bias_bf[:], in_=b_ae.rearrange("(p j) -> p j", j=PACK))
         x_all = keep.tile([P, TILES, A], BF16)
 
         def load_actions(c):
@@ -97,10 +97,10 @@ def tile_actionbindingattention_pa_kernel(tc, actions, W_ae, b_ae, ln_g, ln_b, W
         for c in range(2, len(LOAD_TILES)):
             load_actions(c)
 
-        ident_f32 = keep.tile([P, P], F32)
-        make_identity(nc, ident_f32[:])
         ident_bf = keep.tile([P, P], BF16)
         make_identity(nc, ident_bf[:])
+        ident_f32 = keep.tile([P, P], F32)
+        make_identity(nc, ident_f32[:])
         eps = keep.tile([P, 1], F32)
         nc.vector.memset(eps[:], LN_EPS)
         table_warmer = keep.tile([P, 1], F32)
@@ -108,11 +108,7 @@ def tile_actionbindingattention_pa_kernel(tc, actions, W_ae, b_ae, ln_g, ln_b, W
 
         bias_cols = keep.tile([P, PACK, P], F32)
         nc.vector.tensor_copy(out=bias_cols[:], in_=bias_bf[:].unsqueeze(2).to_broadcast([P, PACK, P]))
-        bias_ps = ps_a.tile([P, F], F32, tag="a_ps")
-        for j in range(PACK):
-            nc.tensor.transpose(out=bias_ps[:, block(j)], in_=bias_cols[:, j, :], identity=ident_f32[:])
         bias_bc = keep.tile([P, F], F32)
-        nc.scalar.copy(out=bias_bc[:], in_=bias_ps[:])
 
         w_aeT_ps = ps_t.tile([P, F], BF16, tag="turned")
         for j in range(PACK):
@@ -125,6 +121,12 @@ def tile_actionbindingattention_pa_kernel(tc, actions, W_ae, b_ae, ln_g, ln_b, W
         wv_grouped = keep.tile([P, O, PACK], BF16, align_bytes=64)
         wv_codes = keep.tile([P, O], U32, align_bytes=64)
         wv_scales = keep.tile([P, O], U8, align_bytes=64)
+
+        def spread_bias():
+            bias_ps = ps_a.tile([P, F], F32, tag="a_ps")
+            for j in range(PACK):
+                nc.tensor.transpose(out=bias_ps[:, block(j)], in_=bias_cols[:, j, :], identity=ident_f32[:])
+            nc.scalar.copy(out=bias_bc[:], in_=bias_ps[:])
 
         def widen_gain_shift():
             nc.vector.tensor_copy(out=gain[:], in_=gain_bf[:])
@@ -320,6 +322,8 @@ def tile_actionbindingattention_pa_kernel(tc, actions, W_ae, b_ae, ln_g, ln_b, W
             g = group_due(step, TURN_LAG)
             if g is not None:
                 transpose_actions(g)
+            if step == TURN_LAG:
+                spread_bias()
             i = tile_due(step, SQUARE_LAG)
             if i is not None:
                 square(i)

@@ -27,15 +27,15 @@ LOAD_TILES = (4, 4, 8, 16, 16, 16)
 RUN = 4
 LN_EPS = 1e-5
 
-TURN_LAG = -3
+TURN_LAG = -5
 ENCODE_LAG = -1
-SQUARE_LAG = 1
+SQUARE_LAG = 2
 DEVIATION_LAG = SQUARE_LAG + GROUP - 1
-NORMALISE_LAG = DEVIATION_LAG + 2
+NORMALISE_LAG = DEVIATION_LAG + 3
 FLIP_LAG = NORMALISE_LAG + 3
 REGROUP_LAG = FLIP_LAG + 3
-QUANTISE_LAG = NORMALISE_LAG + 4 * GROUP
-PROJECT_LAG = QUANTISE_LAG + 2
+QUANTISE_LAG = REGROUP_LAG + GROUP
+PROJECT_LAG = QUANTISE_LAG + 3
 STEPS = TILES + PROJECT_LAG
 VECTOR_BANKS = (1,)
 SCALAR_GROUPS = 2
@@ -70,9 +70,7 @@ def tile_actionbindingattention_pa_kernel(tc, actions, W_ae, b_ae, ln_g, ln_b, W
         work = ctx.enter_context(tc.tile_pool(name="work", bufs=4))
         small = ctx.enter_context(tc.tile_pool(name="small", bufs=6))
         results = ctx.enter_context(tc.tile_pool(name="results", bufs=8))
-        ps_a = ctx.enter_context(tc.psum_pool(name="ps_a", bufs=2))
-        ps_t = ctx.enter_context(tc.psum_pool(name="ps_t", bufs=3))
-        ps_o = ctx.enter_context(tc.psum_pool(name="ps_o", bufs=3))
+        psum = ctx.enter_context(tc.psum_pool(name="psum", bufs=8))
         ctx.enter_context(tc.manual_schedule())
 
         w_ae_sb = keep.tile([P, PACK, A], BF16)
@@ -110,7 +108,7 @@ def tile_actionbindingattention_pa_kernel(tc, actions, W_ae, b_ae, ln_g, ln_b, W
         nc.vector.tensor_copy(out=bias_cols[:], in_=bias_bf[:].unsqueeze(2).to_broadcast([P, PACK, P]))
         bias_bc = keep.tile([P, F], F32)
 
-        w_aeT_ps = ps_t.tile([P, F], BF16, tag="turned")
+        w_aeT_ps = psum.tile([P, F], BF16, tag="bank")
         for j in range(PACK):
             nc.tensor.transpose(out=w_aeT_ps[:, block(j)], in_=w_ae_sb[:, j, :], identity=ident_bf[:])
         w_aeT = keep.tile([P, F], BF16)
@@ -123,7 +121,7 @@ def tile_actionbindingattention_pa_kernel(tc, actions, W_ae, b_ae, ln_g, ln_b, W
         wv_scales = keep.tile([P, O], U8, align_bytes=64)
 
         def spread_bias():
-            bias_ps = ps_a.tile([P, F], F32, tag="a_ps")
+            bias_ps = psum.tile([P, F], F32, tag="bank")
             for j in range(PACK):
                 nc.tensor.transpose(out=bias_ps[:, block(j)], in_=bias_cols[:, j, :], identity=ident_f32[:])
             nc.scalar.copy(out=bias_bc[:], in_=bias_ps[:])
@@ -133,7 +131,7 @@ def tile_actionbindingattention_pa_kernel(tc, actions, W_ae, b_ae, ln_g, ln_b, W
             nc.vector.tensor_copy(out=shift[:], in_=shift_bf[:])
 
         def transpose_wv(b):
-            wvT_ps = ps_t.tile([P, PACK, P], BF16, tag="turned")
+            wvT_ps = psum.tile([P, PACK, P], BF16, tag="bank")
             planes = wv_sb[:, b, :].rearrange("r (p j) -> r j p", j=PACK)
             for j in range(PACK):
                 nc.tensor.transpose(out=wvT_ps[:, j, :], in_=planes[:, j, :], identity=ident_bf[:])
@@ -154,7 +152,7 @@ def tile_actionbindingattention_pa_kernel(tc, actions, W_ae, b_ae, ln_g, ln_b, W
         a_n_planes, a_n_grouped, a_n_codes, a_n_scales, out_psum = {}, {}, {}, {}, {}
 
         def transpose_actions(g):
-            xT_ps = ps_t.tile([P, GROUP_TOKENS], BF16, tag="turned")
+            xT_ps = psum.tile([P, GROUP_TOKENS], BF16, tag="bank")
             for n in range(GROUP):
                 nc.tensor.transpose(out=xT_ps[:, block(n)], in_=x_all[:, g * GROUP + n, :], identity=ident_bf[:])
             xT_sb = work.tile([P, GROUP_TOKENS], BF16)
@@ -163,7 +161,7 @@ def tile_actionbindingattention_pa_kernel(tc, actions, W_ae, b_ae, ln_g, ln_b, W
 
         def encode(i):
             g, n = divmod(i, GROUP)
-            a_ps = ps_a.tile([P, F], F32)
+            a_ps = psum.tile([P, F], F32, tag="bank")
             nc.tensor.matmul(out=a_ps[:], lhsT=xT[g][:, block(n)], rhs=w_aeT[:], start=True, stop=True)
             a_psum[i] = a_ps
 
@@ -234,7 +232,7 @@ def tile_actionbindingattention_pa_kernel(tc, actions, W_ae, b_ae, ln_g, ln_b, W
             if k == 0:
                 planes_tile = work.tile([P, PACK, GROUP_TOKENS], BF16)
                 a_n_planes[g] = planes_tile
-            zT_ps = ps_t.tile([P, BANK_PLANES, GROUP_TOKENS], F32, tag="turned")
+            zT_ps = psum.tile([P, BANK_PLANES, GROUP_TOKENS], F32, tag="bank")
             for b in range(BANK_PLANES):
                 for n in range(GROUP):
                     nc.tensor.transpose(
@@ -283,7 +281,7 @@ def tile_actionbindingattention_pa_kernel(tc, actions, W_ae, b_ae, ln_g, ln_b, W
 
         def project(i):
             g, n = divmod(i, GROUP)
-            out_ps = ps_o.tile([P, O], F32)
+            out_ps = psum.tile([P, O], F32, tag="bank")
             nc.tensor.matmul_mx(
                 out=out_ps[:],
                 lhsT=a_n_codes[g][:, block(n)].bitcast(FP8X4),
@@ -304,18 +302,21 @@ def tile_actionbindingattention_pa_kernel(tc, actions, W_ae, b_ae, ln_g, ln_b, W
             nc.sync.dma_start(out=out_dram[:, i, :], in_=out_sb[:])
 
         for step in range(TURN_LAG, STEPS):
-            g = group_due(step, REGROUP_LAG)
-            if g is not None:
-                regroup(g)
             g = group_due(step, QUANTISE_LAG)
             if g is not None:
                 quantise(g)
-            g = group_due(step, NORMALISE_LAG)
-            if g is not None:
-                centre(g)
             i = tile_due(step, PROJECT_LAG)
             if i is not None:
                 project(i)
+            g = group_due(step, NORMALISE_LAG)
+            if g is not None:
+                centre(g)
+            g = group_due(step, REGROUP_LAG)
+            if g is not None:
+                regroup(g)
+            i = tile_due(step, PROJECT_LAG)
+            if i is not None:
+                store(i)
             i = tile_due(step, 0)
             if i is not None:
                 add_bias(i)
@@ -327,9 +328,6 @@ def tile_actionbindingattention_pa_kernel(tc, actions, W_ae, b_ae, ln_g, ln_b, W
             i = tile_due(step, SQUARE_LAG)
             if i is not None:
                 square(i)
-            i = tile_due(step, PROJECT_LAG)
-            if i is not None:
-                store(i)
             i = tile_due(step, FLIP_LAG)
             if i is not None:
                 flip(i // GROUP, i % GROUP)

@@ -24,7 +24,7 @@ GROUP_TOKENS = GROUP * P
 BANK = 512
 BANK_PLANES = BANK // GROUP_TOKENS
 LOAD_TILES = (4, 4, 8, 16, 16, 16)
-RUN = 4
+RUN = 8
 LN_EPS = 1e-5
 
 TURN_LAG = -5
@@ -69,7 +69,7 @@ def tile_actionbindingattention_pa_kernel(tc, actions, W_ae, b_ae, ln_g, ln_b, W
         keep = ctx.enter_context(tc.tile_pool(name="keep", bufs=1))
         work = ctx.enter_context(tc.tile_pool(name="work", bufs=4))
         small = ctx.enter_context(tc.tile_pool(name="small", bufs=6))
-        results = ctx.enter_context(tc.tile_pool(name="results", bufs=8))
+        results = ctx.enter_context(tc.tile_pool(name="results", bufs=16))
         psum = ctx.enter_context(tc.psum_pool(name="psum", bufs=8))
         ctx.enter_context(tc.manual_schedule())
 

from contextlib import ExitStack

import concourse.mybir as mybir
from concourse.masks import make_identity

BF16 = mybir.dt.bfloat16
F32 = mybir.dt.float32
U32 = mybir.dt.uint32
U8 = mybir.dt.uint8
FP8X4 = mybir.dt.float8_e4m3fn_x4
ACT = mybir.ActivationFunctionType
ALU = mybir.AluOpType

P = 128
PACK = 4
TOKENS = 64 * 128
A = 128
F = 512
O = 512
TILES = TOKENS // P
GROUP = 2
GROUPS = TILES // GROUP
GROUP_TOKENS = GROUP * P
BANK = 512
BANK_PLANES = BANK // GROUP_TOKENS
LOAD_TILES = (4, 4, 8, 16, 16, 16)
RUN = 8
LN_EPS = 1e-5

TURN_LAG = -5
ENCODE_LAG = -1
SQUARE_LAG = 2
DEVIATION_LAG = SQUARE_LAG + GROUP - 1
NORMALISE_LAG = DEVIATION_LAG + 3
FLIP_LAG = NORMALISE_LAG + 3
REGROUP_LAG = FLIP_LAG + 3
QUANTISE_LAG = REGROUP_LAG + GROUP
PROJECT_LAG = QUANTISE_LAG + 3
STEPS = TILES + PROJECT_LAG
VECTOR_BANKS = (1,)
SCALAR_GROUPS = 2
VECTOR_OUTPUTS = 16
PREPARE_STEP = 3
SCALAR_WV = (0, 2)

FLOPS = 2 * TOKENS * A * F + 2 * TOKENS * F * O


def block(i):
    return slice(i * P, (i + 1) * P)


def tile_due(step, lag):
    i = step - lag
    return i if 0 <= i < TILES else None


def group_due(step, lag):
    i = tile_due(step, lag)
    return i // GROUP if i is not None and i % GROUP == 0 else None


def tile_actionbindingattention_pa_kernel(tc, actions, W_ae, b_ae, ln_g, ln_b, Wv, out):
    nc = tc.nc
    x_dram = actions.flatten_outer_dims().rearrange("(p n) a -> p n a", n=TILES)
    out_dram = out.flatten_outer_dims().rearrange("(p n) o -> p n o", n=TILES)

    with ExitStack() as ctx:
        keep = ctx.enter_context(tc.tile_pool(name="keep", bufs=1))
        work = ctx.enter_context(tc.tile_pool(name="work", bufs=4))
        small = ctx.enter_context(tc.tile_pool(name="small", bufs=6))
        results = ctx.enter_context(tc.tile_pool(name="results", bufs=16))
        psum = ctx.enter_context(tc.psum_pool(name="psum", bufs=8))
        ctx.enter_context(tc.manual_schedule())

        w_ae_sb = keep.tile([P, PACK, A], BF16)
        nc.sync.dma_start(out=w_ae_sb[:], in_=W_ae.rearrange("(p j) a -> p j a", j=PACK))
        bias_bf = keep.tile([P, PACK], BF16)
        nc.sync.dma_start(out=bias_bf[:], in_=b_ae.rearrange("(p j) -> p j", j=PACK))
        x_all = keep.tile([P, TILES, A], BF16)

        def load_actions(c):
            first = sum(LOAD_TILES[:c])
            rows = slice(first, first + LOAD_TILES[c])
            nc.sync.dma_start(out=x_all[:, rows, :], in_=x_dram[:, rows, :])

        load_actions(0)
        gain_bf = keep.tile([P, PACK], BF16)
        nc.sync.dma_start(out=gain_bf[:], in_=ln_g.rearrange("(p j) -> p j", j=PACK))
        shift_bf = keep.tile([P, PACK], BF16)
        nc.sync.dma_start(out=shift_bf[:], in_=ln_b.rearrange("(p j) -> p j", j=PACK))
        load_actions(1)
        wv_sb = keep.tile([P, O // P, F], BF16)
        nc.sync.dma_start(out=wv_sb[:], in_=Wv.rearrange("(b r) f -> r b f", r=P))
        for c in range(2, len(LOAD_TILES)):
            load_actions(c)

        ident_bf = keep.tile([P, P], BF16)
        make_identity(nc, ident_bf[:])
        ident_f32 = keep.tile([P, P], F32)
        make_identity(nc, ident_f32[:])
        eps = keep.tile([P, 1], F32)
        nc.vector.memset(eps[:], LN_EPS)
        table_warmer = keep.tile([P, 1], F32)
        nc.scalar.activation(out=table_warmer[:], in_=eps[:], func=ACT.Abs_reciprocal_sqrt)

        bias_cols = keep.tile([P, PACK, P], F32)
        nc.vector.tensor_copy(out=bias_cols[:], in_=bias_bf[:].unsqueeze(2).to_broadcast([P, PACK, P]))
        bias_bc = keep.tile([P, F], F32)

        w_aeT_ps = psum.tile([P, F], BF16, tag="bank")
        for j in range(PACK):
            nc.tensor.transpose(out=w_aeT_ps[:, block(j)], in_=w_ae_sb[:, j, :], identity=ident_bf[:])
        w_aeT = keep.tile([P, F], BF16)
        nc.vector.tensor_copy(out=w_aeT[:], in_=w_aeT_ps[:])

        gain = keep.tile([P, PACK], F32)
        shift = keep.tile([P, PACK], F32)
        wv_grouped = keep.tile([P, O, PACK], BF16, align_bytes=64)
        wv_codes = keep.tile([P, O], U32, align_bytes=64)
        wv_scales = keep.tile([P, O], U8, align_bytes=64)

        def spread_bias():
            bias_ps = psum.tile([P, F], F32, tag="bank")
            for j in range(PACK):
                nc.tensor.transpose(out=bias_ps[:, block(j)], in_=bias_cols[:, j, :], identity=ident_f32[:])
            nc.scalar.copy(out=bias_bc[:], in_=bias_ps[:])

        def widen_gain_shift():
            nc.vector.tensor_copy(out=gain[:], in_=gain_bf[:])
            nc.vector.tensor_copy(out=shift[:], in_=shift_bf[:])

        def transpose_wv(b):
            wvT_ps = psum.tile([P, PACK, P], BF16, tag="bank")
            planes = wv_sb[:, b, :].rearrange("r (p j) -> r j p", j=PACK)
            for j in range(PACK):
                nc.tensor.transpose(out=wvT_ps[:, j, :], in_=planes[:, j, :], identity=ident_bf[:])
            by_word = wvT_ps[:].rearrange("p j o -> p o j")
            if b in SCALAR_WV:
                nc.scalar.copy(out=wv_grouped[:, block(b), :], in_=by_word)
            else:
                nc.vector.tensor_copy(out=wv_grouped[:, block(b), :], in_=by_word)

        def quantise_wv():
            nc.vector.quantize_mx(
                out=wv_codes[:].bitcast(FP8X4),
                scales=wv_scales[:],
                in_=wv_grouped[:].rearrange("p o j -> p (o j)"),
            )

        xT, a_psum, a_sb, a_sum, dev_sq_sum, rstd, neg_mean_rstd, z_sb = {}, {}, {}, {}, {}, {}, {}, {}
        a_n_planes, a_n_grouped, a_n_codes, a_n_scales, out_psum = {}, {}, {}, {}, {}

        def transpose_actions(g):
            xT_ps = psum.tile([P, GROUP_TOKENS], BF16, tag="bank")
            for n in range(GROUP):
                nc.tensor.transpose(out=xT_ps[:, block(n)], in_=x_all[:, g * GROUP + n, :], identity=ident_bf[:])
            xT_sb = work.tile([P, GROUP_TOKENS], BF16)
            nc.scalar.copy(out=xT_sb[:], in_=xT_ps[:])
            xT[g] = xT_sb

        def encode(i):
            g, n = divmod(i, GROUP)
            a_ps = psum.tile([P, F], F32, tag="bank")
            nc.tensor.matmul(out=a_ps[:], lhsT=xT[g][:, block(n)], rhs=w_aeT[:], start=True, stop=True)
            a_psum[i] = a_ps

        def add_bias(i):
            g, n = divmod(i, GROUP)
            if n == 0:
                a_tile = work.tile([P, GROUP, F], F32)
                a_sb[g] = a_tile
                sum_tile = small.tile([P, GROUP], F32)
                a_sum[g] = sum_tile
            nc.vector.scalar_tensor_tensor(
                out=a_sb[g][:, n, :],
                in0=a_psum[i][:],
                scalar=1.0,
                in1=bias_bc[:],
                op0=ALU.mult,
                op1=ALU.add,
                accum_out=a_sum[g][:, n : n + 1],
            )

        def square(i):
            g, n = divmod(i, GROUP)
            if n == 0:
                sq_tile = small.tile([P, GROUP], F32)
                dev_sq_sum[g] = sq_tile
            dev_sq = work.tile([P, F], BF16)
            nc.scalar.activation(
                out=dev_sq[:],
                in_=a_sb[g][:, n, :],
                func=ACT.Square,
                bias=a_sum[g][:, n : n + 1],
                scale=-1.0 * F,
                accum_out=dev_sq_sum[g][:, n : n + 1],
            )

        def deviation(g):
            rstd_tile = small.tile([P, GROUP], F32)
            nc.scalar.activation(
                out=rstd_tile[:],
                in_=dev_sq_sum[g][:],
                func=ACT.Abs_reciprocal_sqrt,
                bias=eps[:],
                scale=1.0 / (F * F * F),
            )
            rstd[g] = rstd_tile

        def centre(g):
            centre_tile = small.tile([P, GROUP], F32)
            nc.vector.scalar_tensor_tensor(
                out=centre_tile[:], in0=a_sum[g][:], scalar=-1.0 / F, in1=rstd[g][:], op0=ALU.mult, op1=ALU.mult
            )
            neg_mean_rstd[g] = centre_tile

        def normalise(g):
            z_tile = work.tile([P, GROUP, F], F32)
            for n in range(GROUP):
                nc.gpsimd.tensor_scalar(
                    out=z_tile[:, n, :],
                    in0=a_sb[g][:, n, :],
                    scalar1=rstd[g][:, n : n + 1],
                    scalar2=neg_mean_rstd[g][:, n : n + 1],
                    op0=ALU.mult,
                    op1=ALU.add,
                )
            z_sb[g] = z_tile

        def flip(g, k):
            if k == 0:
                planes_tile = work.tile([P, PACK, GROUP_TOKENS], BF16)
                a_n_planes[g] = planes_tile
            zT_ps = psum.tile([P, BANK_PLANES, GROUP_TOKENS], F32, tag="bank")
            for b in range(BANK_PLANES):
                for n in range(GROUP):
                    nc.tensor.transpose(
                        out=zT_ps[:, b, block(n)],
                        in_=z_sb[g][:, n, block(k * BANK_PLANES + b)],
                        identity=ident_f32[:],
                    )
            for b in range(BANK_PLANES):
                j = k * BANK_PLANES + b
                if k in VECTOR_BANKS and g >= SCALAR_GROUPS:
                    nc.vector.tensor_scalar(
                        out=a_n_planes[g][:, j, :],
                        in0=zT_ps[:, b, :],
                        scalar1=gain[:, j : j + 1],
                        scalar2=shift[:, j : j + 1],
                        op0=ALU.mult,
                        op1=ALU.add,
                    )
                else:
                    nc.scalar.activation(
                        out=a_n_planes[g][:, j, :],
                        in_=zT_ps[:, b, :],
                        func=ACT.Identity,
                        scale=gain[:, j : j + 1],
                        bias=shift[:, j : j + 1],
                    )

        def regroup(g):
            grouped_tile = work.tile([P, GROUP_TOKENS, PACK], BF16, align_bytes=64)
            nc.vector.tensor_copy(
                out=grouped_tile[:].rearrange("p (c i) j -> p c j i", i=RUN),
                in_=a_n_planes[g][:].rearrange("p j (c i) -> p c j i", i=RUN),
            )
            a_n_grouped[g] = grouped_tile

        def quantise(g):
            codes_tile = work.tile([P, GROUP_TOKENS], U32, align_bytes=64)
            scales_tile = work.tile([P, GROUP_TOKENS], U8, align_bytes=64)
            nc.vector.quantize_mx(
                out=codes_tile[:].bitcast(FP8X4),
                scales=scales_tile[:],
                in_=a_n_grouped[g][:].rearrange("p c j -> p (c j)"),
            )
            a_n_codes[g] = codes_tile
            a_n_scales[g] = scales_tile

        def project(i):
            g, n = divmod(i, GROUP)
            out_ps = psum.tile([P, O], F32, tag="bank")
            nc.tensor.matmul_mx(
                out=out_ps[:],
                lhsT=a_n_codes[g][:, block(n)].bitcast(FP8X4),
                lhsT_scale=a_n_scales[g][:, block(n)],
                rhs=wv_codes[:].bitcast(FP8X4),
                rhs_scale=wv_scales[:],
                start=True,
                stop=True,
            )
            out_psum[i] = out_ps

        def store(i):
            out_sb = results.tile([P, O], F32)
            if i % VECTOR_OUTPUTS == VECTOR_OUTPUTS - 1:
                nc.vector.tensor_copy(out=out_sb[:], in_=out_psum[i][:])
            else:
                nc.scalar.copy(out=out_sb[:], in_=out_psum[i][:])
            nc.sync.dma_start(out=out_dram[:, i, :], in_=out_sb[:])

        for step in range(TURN_LAG, STEPS):
            g = group_due(step, QUANTISE_LAG)
            if g is not None:
                quantise(g)
            i = tile_due(step, PROJECT_LAG)
            if i is not None:
                project(i)
            g = group_due(step, NORMALISE_LAG)
            if g is not None:
                centre(g)
            g = group_due(step, REGROUP_LAG)
            if g is not None:
                regroup(g)
            i = tile_due(step, PROJECT_LAG)
            if i is not None:
                store(i)
            i = tile_due(step, 0)
            if i is not None:
                add_bias(i)
            g = group_due(step, TURN_LAG)
            if g is not None:
                transpose_actions(g)
            if step == TURN_LAG:
                spread_bias()
            i = tile_due(step, SQUARE_LAG)
            if i is not None:
                square(i)
            i = tile_due(step, FLIP_LAG)
            if i is not None:
                flip(i // GROUP, i % GROUP)
            g = group_due(step, DEVIATION_LAG)
            if g is not None:
                deviation(g)
            g = group_due(step, NORMALISE_LAG)
            if g is not None:
                normalise(g)
            i = tile_due(step, ENCODE_LAG)
            if i is not None:
                encode(i)
            b = step - PREPARE_STEP
            if b == 0:
                widen_gain_shift()
            if 0 <= b < O // P:
                transpose_wv(b)
            if b == O // P:
                quantise_wv()
